import numpy as np
import ml_dtypes


def mxq(x, axis, fmt="e4m3"):
    dtype, down = {"e4m3": (ml_dtypes.float8_e4m3fn, 7), "e5m2": (ml_dtypes.float8_e5m2, 14)}[fmt]
    v = np.moveaxis(np.asarray(x, np.float32).astype(ml_dtypes.bfloat16).astype(np.float64), axis, -1)
    blocks = v.reshape(v.shape[:-1] + (-1, 32))
    amax = np.abs(blocks).max(-1, keepdims=True)
    byte = np.maximum(np.where(amax > 0, np.frexp(amax)[1] - 1 + 127, 0) - down, 1)
    scale = np.exp2(byte - 127.0)
    codes = (blocks / scale).astype(np.float32).astype(dtype).astype(np.float64)
    return np.moveaxis((codes * scale).reshape(v.shape), -1, axis)


WIDE = False


def mx_kscale(k):
    if not WIDE:
        return np.ones(k)
    levels = np.array([10, -10, 5, -5, 0])
    if k % 512:
        return np.exp2(np.random.permutation(np.resize(levels, k // 32))).repeat(32)
    a = np.empty((k // 512, 16))
    for p in range(k // 512):
        a[p, :8] = np.random.permutation(np.resize(levels, 8))
        for g in range(8):
            far = levels[np.abs(levels - a[p, g]) >= 10]
            a[p, g + 8] = far[np.random.randint(len(far))]
    return np.exp2(a.ravel()).repeat(32)


BF16 = ml_dtypes.bfloat16


def bf(x):
    return np.asarray(x, np.float32).astype(BF16)


def f64(x):
    return np.asarray(x).astype(np.float64)


B, S, D_MODEL, N_HEADS, QK_ROPE, QK_NOPE, KV_LORA, V_DIM = 4, 2048, 1024, 2, 32, 32, 512, 128
QK_DIM = QK_ROPE + QK_NOPE
ROPE_BASE = 10000.0


def apply_rope(r):
    freqs = 1.0 / (ROPE_BASE ** (np.arange(0, QK_ROPE, 2) / QK_ROPE))
    t = np.arange(S)[:, None] * freqs[None, :]
    cos = np.cos(t)[None, :, None, :]
    sin = np.sin(t)[None, :, None, :]
    r1 = r[..., 0::2]
    r2 = r[..., 1::2]
    return np.stack([r1 * cos - r2 * sin, r2 * cos + r1 * sin], axis=-1).reshape(r.shape)


def setup_inputs():
    s = mx_kscale(D_MODEL)
    return {"x": bf(np.random.standard_normal((B, S, D_MODEL)) * s),
            "Wq": bf(np.random.standard_normal((D_MODEL, N_HEADS * QK_DIM)) / np.sqrt(D_MODEL) / s[:, None])}


def reference(x, Wq):
    q = (mxq(f64(x), 2, "e4m3") @ mxq(f64(Wq), 0, "e4m3")).reshape(B, S, N_HEADS, QK_DIM)
    q_nope, q_rope = q[..., :QK_NOPE], q[..., QK_NOPE:]
    return np.concatenate([q_nope, apply_rope(q_rope)], axis=-1)

@@ -1,0 +1,266 @@
+from contextlib import ExitStack
+
+import concourse.mybir as mybir
+from concourse.masks import make_identity
+
+F32 = mybir.dt.float32
+BF16 = mybir.dt.bfloat16
+I32 = mybir.dt.int32
+U32 = mybir.dt.uint32
+U8 = mybir.dt.uint8
+FP8X4 = mybir.dt.float8_e4m3fn_x4
+ALU = mybir.AluOpType
+ACTF = mybir.ActivationFunctionType
+
+P = 128
+BATCH = 4
+SEQ = 2048
+D_MODEL = 1024
+FEATS = 128
+HEADS = 2
+HEAD_DIM = 64
+NOPE = 32
+PAIRS = 16
+SLOTS = 16
+ROUND = 4
+WORDS = D_MODEL // 2
+PI = 3.141592653589793
+ROPE_BASE = 10000.0
+
+FLOPS = 2 * BATCH * SEQ * D_MODEL * FEATS
+
+
+def split_turns():
+    his = []
+    los = []
+    for i in range(PAIRS):
+        g = ROPE_BASE ** (-i / 16.0) / (2.0 * PI)
+        unit = 1.0
+        for step in range(64):
+            if g * unit < 4096.0:
+                unit = unit * 2.0
+        hi = round(g * unit) / unit
+        his.append(hi)
+        los.append(g - hi)
+    return his, los
+
+
+def tile_multiheadlatentattention_pb_t_kernel(tc, x, Wq, out):
+    nc = tc.nc
+    with ExitStack() as ctx:
+        const = ctx.enter_context(tc.tile_pool(name="const", bufs=1))
+        xpool = ctx.enter_context(tc.tile_pool(name="xin", bufs=1))
+        opool = ctx.enter_context(tc.tile_pool(name="res", bufs=1))
+        gpool = ctx.enter_context(tc.tile_pool(name="grp", bufs=3))
+        qpool = ctx.enter_context(tc.tile_pool(name="quant", bufs=3))
+        vpool = ctx.enter_context(tc.tile_pool(name="vtmp", bufs=3))
+        psx = ctx.enter_context(tc.psum_pool(name="psx", bufs=6))
+        psa = ctx.enter_context(tc.psum_pool(name="psa", bufs=2))
+        ctx.enter_context(tc.manual_schedule())
+
+        w_raw = const.tile([P, 2, 4 * FEATS], BF16, name="w_raw")
+
+        chunks = [(0, 0, 1), (0, 1, 1), (0, 2, 2), (0, 4, 4), (0, 8, 4), (0, 12, 4)]
+        for b in range(1, BATCH):
+            for j0 in range(0, SLOTS, 4):
+                chunks.append((b, j0, 4))
+        where = {}
+        for b, j0, nj in chunks:
+            xs = xpool.tile([P, nj * D_MODEL], BF16, name="x%d_%d" % (b, j0))
+            nc.sync.dma_start(
+                out=xs[:].rearrange("p (j k) -> p j k", k=D_MODEL),
+                in_=x[b].rearrange("(p j) k -> p j k", j=SLOTS)[:, j0 : j0 + nj, :],
+            )
+            for jj in range(nj):
+                where[(b, j0 + jj)] = (xs, jj)
+            if (b, j0) == (0, 1):
+                nc.sync.dma_start(out=w_raw[:], in_=Wq.rearrange("(g q t) c -> q g (t c)", g=2, t=4))
+
+        zero = const.tile([P, 1], F32, name="zero")
+        warm = const.tile([P, 1], F32, name="warm")
+        nc.vector.memset(zero[:], 0.0)
+        nc.scalar.activation(out=warm[:], in_=zero[:], func=ACTF.Sin)
+
+        pos = const.tile([P, SLOTS], F32, name="pos")
+        nc.gpsimd.iota(
+            pos[:], pattern=[[1, SLOTS]], base=0, channel_multiplier=SLOTS,
+            allow_small_or_imprecise_dtypes=True,
+        )
+        ident = const.tile([P, P], F32, name="ident")
+        make_identity(nc, ident[:])
+
+        his, los = split_turns()
+        g_hi = const.tile([P, PAIRS], F32, name="g_hi")
+        for i in range(PAIRS):
+            nc.vector.memset(g_hi[:, i : i + 1], his[i])
+
+        full = [P, SLOTS, PAIRS]
+        t_hi = const.tile(full, F32, name="t_hi")
+        t_lo = const.tile(full, F32, name="t_lo")
+        k_int = const.tile(full, I32, name="k_int")
+        k_f = const.tile(full, F32, name="k_f")
+        frac = const.tile(full, F32, name="frac")
+        quarter = const.tile(full, F32, name="quarter")
+        nc.vector.tensor_tensor(
+            out=t_hi[:], in0=pos[:].unsqueeze(2).to_broadcast(full),
+            in1=g_hi[:].unsqueeze(1).to_broadcast(full), op=ALU.mult,
+        )
+        for i in range(PAIRS):
+            nc.vector.tensor_scalar(
+                out=t_lo[:, :, i], in0=pos[:], scalar1=los[i], scalar2=None, op0=ALU.mult
+            )
+        nc.vector.tensor_scalar(out=k_int[:], in0=t_hi[:], scalar1=-0.2, scalar2=None, op0=ALU.add)
+        nc.vector.tensor_copy(out=k_f[:], in_=k_int[:])
+        nc.vector.tensor_tensor(out=frac[:], in0=t_hi[:], in1=k_f[:], op=ALU.subtract)
+        nc.vector.tensor_tensor(out=frac[:], in0=frac[:], in1=t_lo[:], op=ALU.add)
+
+        w_grp = const.tile([P, 2, FEATS, 4], BF16, name="w_grp", align_bytes=64)
+        w_codes = const.tile([P, 2 * FEATS], U32, name="w_codes", align_bytes=64)
+        w_scales = const.tile([P, 2 * FEATS], U8, name="w_scales", align_bytes=64)
+
+        def regroup_w():
+            for g in range(2):
+                nc.scalar.copy(
+                    out=w_grp[:, g, :, :],
+                    in_=w_raw[:, g, :].rearrange("p (t c) -> p c t", t=4),
+                )
+
+        def quantise_w():
+            nc.vector.quantize_mx(
+                out=w_codes[:].bitcast(FP8X4), scales=w_scales[:],
+                in_=w_grp[:].rearrange("p g c t -> p (g c t)"),
+            )
+
+        arg = const.tile([P, 2, SLOTS * PAIRS, 2], F32, name="arg")
+        table = const.tile([P, 2, SLOTS, 2 * PAIRS], F32, name="table")
+        flat = frac[:].rearrange("p j i -> p (j i)")
+        qflat = quarter[:].rearrange("p j i -> p (j i)")
+        nc.vector.scalar_tensor_tensor(
+            out=arg[:, 0, :, 1], in0=flat, scalar=0.5, in1=flat, op0=ALU.is_gt, op1=ALU.subtract
+        )
+        nc.vector.tensor_scalar(out=qflat, in0=flat, scalar1=0.25, scalar2=None, op0=ALU.add)
+        nc.vector.scalar_tensor_tensor(
+            out=arg[:, 0, :, 0], in0=qflat, scalar=0.5, in1=qflat, op0=ALU.is_gt, op1=ALU.subtract
+        )
+        nc.gpsimd.tensor_scalar(
+            out=arg[:, 1, :, 0], in0=arg[:, 0, :, 1], scalar1=-1.0, scalar2=0.0, op0=ALU.mult, op1=ALU.add
+        )
+        nc.gpsimd.tensor_scalar(
+            out=arg[:, 1, :, 1], in0=arg[:, 0, :, 0], scalar1=1.0, scalar2=0.0, op0=ALU.mult, op1=ALU.add
+        )
+
+        def make_table():
+            nc.scalar.activation(
+                out=table[:].rearrange("p a j c -> p (a j c)"),
+                in_=arg[:].rearrange("p a n e -> p (a n e)"),
+                func=ACTF.Sin, scale=-2.0 * PI,
+            )
+
+        results = []
+        for b in range(BATCH):
+            ob = opool.tile([P, SLOTS, FEATS], F32, name="ob%d" % b)
+            results.append(ob)
+
+        units = []
+        for b in range(BATCH):
+            for j0 in range(0, SLOTS, ROUND):
+                units.append((b, j0, ROUND))
+        units = units[:-1] + [(BATCH - 1, 12, 2), (BATCH - 1, 14, 2)]
+        stores = {}
+        for b in range(BATCH - 1):
+            stores[(b, 12)] = (0, SLOTS)
+        stores[(BATCH - 1, 4)] = (0, 8)
+        stores[(BATCH - 1, 8)] = (8, 4)
+        stores[(BATCH - 1, 12)] = (12, 2)
+        stores[(BATCH - 1, 14)] = (14, 2)
+
+        grouped = {}
+        quantised = {}
+
+        def transpose_and_copy(u):
+            b, j0, n = units[u]
+            grp = gpool.tile([P, n * WORDS], F32, name="grp", tag="grp", align_bytes=64)
+            grouped[u] = grp
+            for t in range(n):
+                xs, jj = where[(b, j0 + t)]
+                xw = xs[:].bitcast(F32)
+                xt = psx.tile([P, WORDS], F32, name="xt", tag="xt")
+                for a in range(4):
+                    first = jj * WORDS + (a // 2) * 2 * P + a % 2
+                    nc.tensor.transpose(
+                        xt[:, a * P : (a + 1) * P],
+                        xw[:, first : (jj * WORDS + (a // 2 + 1) * 2 * P) : 2],
+                        ident[:],
+                    )
+                nc.scalar.copy(
+                    out=grp[:, t * WORDS : (t + 1) * WORDS].rearrange("p (g r u) -> p g r u", g=2, u=2),
+                    in_=xt[:].rearrange("p (g u r) -> p g r u", g=2, u=2),
+                )
+                if u == 0 and t == 1:
+                    regroup_w()
+                if u == 2 and t == 1:
+                    make_table()
+
+        def quantise(u):
+            n = units[u][2]
+            codes = qpool.tile([P, n * 2 * P], U32, name="codes", tag="codes", align_bytes=64)
+            scales = qpool.tile([P, n * 2 * P], U8, name="scales", tag="scales", align_bytes=64)
+            nc.vector.quantize_mx(
+                out=codes[:].bitcast(FP8X4), scales=scales[:], in_=grouped[u][:].bitcast(BF16)
+            )
+            quantised[u] = (codes, scales)
+
+        def multiply_and_rotate(u):
+            b, j0, n = units[u]
+            codes, scales = quantised[u]
+            acc = psa.tile([P, n * FEATS], F32, name="acc", tag="acc")
+            for t in range(n):
+                for g in range(2):
+                    cols = slice((2 * t + g) * P, (2 * t + g + 1) * P)
+                    nc.tensor.matmul_mx(
+                        out=acc[:, t * FEATS : (t + 1) * FEATS],
+                        lhsT=codes[:, cols].bitcast(FP8X4),
+                        lhsT_scale=scales[:, cols],
+                        rhs=w_codes[:, g * FEATS : (g + 1) * FEATS].bitcast(FP8X4),
+                        rhs_scale=w_scales[:, g * FEATS : (g + 1) * FEATS],
+                        start=(g == 0),
+                        stop=(g == 1),
+                    )
+            q = acc[:].rearrange("p (t h d) -> p t h d", t=n, h=HEADS)
+            o = results[b][:, j0 : j0 + n, :].rearrange("p t (h d) -> p t h d", h=HEADS)
+            shape = [P, n, HEADS, PAIRS, 2]
+            pairs = q[:, :, :, NOPE:HEAD_DIM].rearrange("p t h (i e) -> p t h i e", e=2)
+            o_rope = o[:, :, :, NOPE:HEAD_DIM].rearrange("p t h (i e) -> p t h i e", e=2)
+            v = vpool.tile(shape, F32, name="v", tag="v")
+            nc.vector.tensor_copy(out=o[:, :, :, 0:NOPE], in_=q[:, :, :, 0:NOPE])
+            nc.vector.tensor_tensor(
+                out=o_rope,
+                in0=pairs[:, :, :, :, 0:1].to_broadcast(shape),
+                in1=table[:, 0, j0 : j0 + n, :].rearrange("p t (i e) -> p t i e", e=2)
+                .unsqueeze(2).to_broadcast(shape),
+                op=ALU.mult,
+            )
+            nc.vector.tensor_tensor(
+                out=v[:],
+                in0=pairs[:, :, :, :, 1:2].to_broadcast(shape),
+                in1=table[:, 1, j0 : j0 + n, :].rearrange("p t (i e) -> p t i e", e=2)
+                .unsqueeze(2).to_broadcast(shape),
+                op=ALU.mult,
+            )
+            nc.gpsimd.tensor_tensor(out=o_rope, in0=o_rope, in1=v[:], op=ALU.add)
+            if (b, j0) in stores:
+                s0, sn = stores[(b, j0)]
+                nc.sync.dma_start(
+                    out=out[b].rearrange("(p j) h d -> p j (h d)", j=SLOTS)[:, s0 : s0 + sn, :],
+                    in_=results[b][:, s0 : s0 + sn, :],
+                )
+
+        for u in range(-2, len(units)):
+            if u + 2 < len(units):
+                transpose_and_copy(u + 2)
+            if u == -2:
+                quantise_w()
+            if 0 <= u + 1 < len(units):
+                quantise(u + 1)
+            if u >= 0:
+                multiply_and_rotate(u)

@@ -22,6 +22,7 @@ HEAD_DIM = 64
 NOPE = 32
 PAIRS = 16
 SLOTS = 16
+REORDERED = 2
 ROUND = 4
 WORDS = D_MODEL // 2
 PI = 3.141592653589793
@@ -53,6 +54,7 @@ def tile_multiheadlatentattention_pb_t_kernel(tc, x, Wq, out):
         opool = ctx.enter_context(tc.tile_pool(name="res", bufs=1))
         gpool = ctx.enter_context(tc.tile_pool(name="grp", bufs=3))
         qpool = ctx.enter_context(tc.tile_pool(name="quant", bufs=3))
+        ppool = ctx.enter_context(tc.tile_pool(name="reord", bufs=3))
         vpool = ctx.enter_context(tc.tile_pool(name="vtmp", bufs=3))
         psx = ctx.enter_context(tc.psum_pool(name="psx", bufs=6))
         psa = ctx.enter_context(tc.psum_pool(name="psa", bufs=2))
@@ -177,6 +179,20 @@ def tile_multiheadlatentattention_pb_t_kernel(tc, x, Wq, out):
         grouped = {}
         quantised = {}
 
+        reordered = {}
+
+        def reorder(u):
+            b, j0, n = units[u]
+            m = REORDERED
+            xs, jj = where[(b, j0 + n - m)]
+            xp = ppool.tile([P, m * WORDS], F32, name="xp", tag="xp", align_bytes=64)
+            nc.vector.tensor_copy(
+                out=xp[:].rearrange("p (g u c) -> p g u c", u=2, c=P),
+                in_=xs[:].bitcast(F32)[:, jj * WORDS : (jj + m) * WORDS].rearrange("p (g c u) -> p g u c", u=2, c=P),
+            )
+            for t in range(m):
+                reordered[(u, n - m + t)] = (xp, t)
+
         def transpose_and_copy(u):
             b, j0, n = units[u]
             grp = gpool.tile([P, n * WORDS], F32, name="grp", tag="grp", align_bytes=64)
@@ -186,12 +202,13 @@ def tile_multiheadlatentattention_pb_t_kernel(tc, x, Wq, out):
                 xw = xs[:].bitcast(F32)
                 xt = psx.tile([P, WORDS], F32, name="xt", tag="xt")
                 for a in range(4):
-                    first = jj * WORDS + (a // 2) * 2 * P + a % 2
-                    nc.tensor.transpose(
-                        xt[:, a * P : (a + 1) * P],
-                        xw[:, first : (jj * WORDS + (a // 2 + 1) * 2 * P) : 2],
-                        ident[:],
-                    )
+                    if (u, t) in reordered:
+                        xp, tp = reordered[(u, t)]
+                        words = xp[:, tp * WORDS + a * P : tp * WORDS + (a + 1) * P]
+                    else:
+                        first = jj * WORDS + (a // 2) * 2 * P + a % 2
+                        words = xw[:, first : (jj * WORDS + (a // 2 + 1) * 2 * P) : 2]
+                    nc.tensor.transpose(xt[:, a * P : (a + 1) * P], words, ident[:])
                 nc.scalar.copy(
                     out=grp[:, t * WORDS : (t + 1) * WORDS].rearrange("p (g r u) -> p g r u", g=2, u=2),
                     in_=xt[:].rearrange("p (g u r) -> p g r u", g=2, u=2),
@@ -262,5 +279,7 @@ def tile_multiheadlatentattention_pb_t_kernel(tc, x, Wq, out):
                 quantise_w()
             if 0 <= u + 1 < len(units):
                 quantise(u + 1)
+            if 3 <= u + 3 < len(units) - 2:
+                reorder(u + 3)
             if u >= 0:
                 multiply_and_rotate(u)

@@ -213,6 +213,8 @@ def tile_multiheadlatentattention_pb_t_kernel(tc, x, Wq, out):
                     out=grp[:, t * WORDS : (t + 1) * WORDS].rearrange("p (g r u) -> p g r u", g=2, u=2),
                     in_=xt[:].rearrange("p (g u r) -> p g r u", g=2, u=2),
                 )
+                if t == 1 and u - 3 >= 0:
+                    pass_through(u - 3)
                 if u == 0 and t == 1:
                     regroup_w()
                 if u == 2 and t == 1:
@@ -226,6 +228,8 @@ def tile_multiheadlatentattention_pb_t_kernel(tc, x, Wq, out):
                 out=codes[:].bitcast(FP8X4), scales=scales[:], in_=grouped[u][:].bitcast(BF16)
             )
             quantised[u] = (codes, scales)
+
+        rotating = {}
 
         def multiply_and_rotate(u):
             b, j0, n = units[u]
@@ -249,7 +253,6 @@ def tile_multiheadlatentattention_pb_t_kernel(tc, x, Wq, out):
             pairs = q[:, :, :, NOPE:HEAD_DIM].rearrange("p t h (i e) -> p t h i e", e=2)
             o_rope = o[:, :, :, NOPE:HEAD_DIM].rearrange("p t h (i e) -> p t h i e", e=2)
             v = vpool.tile(shape, F32, name="v", tag="v")
-            nc.vector.tensor_copy(out=o[:, :, :, 0:NOPE], in_=q[:, :, :, 0:NOPE])
             nc.vector.tensor_tensor(
                 out=o_rope,
                 in0=pairs[:, :, :, :, 0:1].to_broadcast(shape),
@@ -264,7 +267,16 @@ def tile_multiheadlatentattention_pb_t_kernel(tc, x, Wq, out):
                 .unsqueeze(2).to_broadcast(shape),
                 op=ALU.mult,
             )
-            nc.gpsimd.tensor_tensor(out=o_rope, in0=o_rope, in1=v[:], op=ALU.add)
+            rotating[u] = (q, o, o_rope, v)
+
+        def pass_through(u):
+            q, o, o_rope, v = rotating[u]
+            nc.scalar.copy(out=o[:, :, :, 0:NOPE], in_=q[:, :, :, 0:NOPE])
+
+        def add_and_store(u):
+            b, j0, n = units[u]
+            q, o, o_rope, v = rotating[u]
+            nc.vector.tensor_tensor(out=o_rope, in0=o_rope, in1=v[:], op=ALU.add)
             if (b, j0) in stores:
                 s0, sn = stores[(b, j0)]
                 nc.sync.dma_start(
@@ -275,11 +287,17 @@ def tile_multiheadlatentattention_pb_t_kernel(tc, x, Wq, out):
         for u in range(-2, len(units)):
             if u + 2 < len(units):
                 transpose_and_copy(u + 2)
+            elif u >= 1:
+                pass_through(u - 1)
             if u == -2:
                 quantise_w()
             if 0 <= u + 1 < len(units):
                 quantise(u + 1)
+            if u >= 1:
+                add_and_store(u - 1)
             if 3 <= u + 3 < len(units) - 2:
                 reorder(u + 3)
             if u >= 0:
                 multiply_and_rotate(u)
+        pass_through(len(units) - 1)
+        add_and_store(len(units) - 1)

from contextlib import ExitStack

import concourse.mybir as mybir
from concourse.masks import make_identity

F32 = mybir.dt.float32
BF16 = mybir.dt.bfloat16
I32 = mybir.dt.int32
U32 = mybir.dt.uint32
U8 = mybir.dt.uint8
FP8X4 = mybir.dt.float8_e4m3fn_x4
ALU = mybir.AluOpType
ACTF = mybir.ActivationFunctionType

P = 128
BATCH = 4
SEQ = 2048
D_MODEL = 1024
FEATS = 128
HEADS = 2
HEAD_DIM = 64
NOPE = 32
PAIRS = 16
SLOTS = 16
REORDERED = 2
ROUND = 4
WORDS = D_MODEL // 2
PI = 3.141592653589793
ROPE_BASE = 10000.0

FLOPS = 2 * BATCH * SEQ * D_MODEL * FEATS


def split_turns():
    his = []
    los = []
    for i in range(PAIRS):
        g = ROPE_BASE ** (-i / 16.0) / (2.0 * PI)
        unit = 1.0
        for step in range(64):
            if g * unit < 4096.0:
                unit = unit * 2.0
        hi = round(g * unit) / unit
        his.append(hi)
        los.append(g - hi)
    return his, los


def tile_multiheadlatentattention_pb_t_kernel(tc, x, Wq, out):
    nc = tc.nc
    with ExitStack() as ctx:
        const = ctx.enter_context(tc.tile_pool(name="const", bufs=1))
        xpool = ctx.enter_context(tc.tile_pool(name="xin", bufs=1))
        opool = ctx.enter_context(tc.tile_pool(name="res", bufs=1))
        gpool = ctx.enter_context(tc.tile_pool(name="grp", bufs=3))
        qpool = ctx.enter_context(tc.tile_pool(name="quant", bufs=3))
        ppool = ctx.enter_context(tc.tile_pool(name="reord", bufs=3))
        vpool = ctx.enter_context(tc.tile_pool(name="vtmp", bufs=3))
        psx = ctx.enter_context(tc.psum_pool(name="psx", bufs=6))
        psa = ctx.enter_context(tc.psum_pool(name="psa", bufs=2))
        ctx.enter_context(tc.manual_schedule())

        w_raw = const.tile([P, 2, 4 * FEATS], BF16, name="w_raw")

        chunks = [(0, 0, 1), (0, 1, 1), (0, 2, 2), (0, 4, 4), (0, 8, 4), (0, 12, 4)]
        for b in range(1, BATCH):
            for j0 in range(0, SLOTS, 4):
                chunks.append((b, j0, 4))
        where = {}
        for b, j0, nj in chunks:
            xs = xpool.tile([P, nj * D_MODEL], BF16, name="x%d_%d" % (b, j0))
            nc.sync.dma_start(
                out=xs[:].rearrange("p (j k) -> p j k", k=D_MODEL),
                in_=x[b].rearrange("(p j) k -> p j k", j=SLOTS)[:, j0 : j0 + nj, :],
            )
            for jj in range(nj):
                where[(b, j0 + jj)] = (xs, jj)
            if (b, j0) == (0, 1):
                nc.sync.dma_start(out=w_raw[:], in_=Wq.rearrange("(g q t) c -> q g (t c)", g=2, t=4))

        zero = const.tile([P, 1], F32, name="zero")
        warm = const.tile([P, 1], F32, name="warm")
        nc.vector.memset(zero[:], 0.0)
        nc.scalar.activation(out=warm[:], in_=zero[:], func=ACTF.Sin)

        pos = const.tile([P, SLOTS], F32, name="pos")
        nc.gpsimd.iota(
            pos[:], pattern=[[1, SLOTS]], base=0, channel_multiplier=SLOTS,
            allow_small_or_imprecise_dtypes=True,
        )
        ident = const.tile([P, P], F32, name="ident")
        make_identity(nc, ident[:])

        his, los = split_turns()
        g_hi = const.tile([P, PAIRS], F32, name="g_hi")
        for i in range(PAIRS):
            nc.vector.memset(g_hi[:, i : i + 1], his[i])

        full = [P, SLOTS, PAIRS]
        t_hi = const.tile(full, F32, name="t_hi")
        t_lo = const.tile(full, F32, name="t_lo")
        k_int = const.tile(full, I32, name="k_int")
        k_f = const.tile(full, F32, name="k_f")
        frac = const.tile(full, F32, name="frac")
        quarter = const.tile(full, F32, name="quarter")
        nc.vector.tensor_tensor(
            out=t_hi[:], in0=pos[:].unsqueeze(2).to_broadcast(full),
            in1=g_hi[:].unsqueeze(1).to_broadcast(full), op=ALU.mult,
        )
        for i in range(PAIRS):
            nc.vector.tensor_scalar(
                out=t_lo[:, :, i], in0=pos[:], scalar1=los[i], scalar2=None, op0=ALU.mult
            )
        nc.vector.tensor_scalar(out=k_int[:], in0=t_hi[:], scalar1=-0.2, scalar2=None, op0=ALU.add)
        nc.vector.tensor_copy(out=k_f[:], in_=k_int[:])
        nc.vector.tensor_tensor(out=frac[:], in0=t_hi[:], in1=k_f[:], op=ALU.subtract)
        nc.vector.tensor_tensor(out=frac[:], in0=frac[:], in1=t_lo[:], op=ALU.add)

        w_grp = const.tile([P, 2, FEATS, 4], BF16, name="w_grp", align_bytes=64)
        w_codes = const.tile([P, 2 * FEATS], U32, name="w_codes", align_bytes=64)
        w_scales = const.tile([P, 2 * FEATS], U8, name="w_scales", align_bytes=64)

        def regroup_w():
            for g in range(2):
                nc.scalar.copy(
                    out=w_grp[:, g, :, :],
                    in_=w_raw[:, g, :].rearrange("p (t c) -> p c t", t=4),
                )

        def quantise_w():
            nc.vector.quantize_mx(
                out=w_codes[:].bitcast(FP8X4), scales=w_scales[:],
                in_=w_grp[:].rearrange("p g c t -> p (g c t)"),
            )

        arg = const.tile([P, 2, SLOTS * PAIRS, 2], F32, name="arg")
        table = const.tile([P, 2, SLOTS, 2 * PAIRS], F32, name="table")
        flat = frac[:].rearrange("p j i -> p (j i)")
        qflat = quarter[:].rearrange("p j i -> p (j i)")
        nc.vector.scalar_tensor_tensor(
            out=arg[:, 0, :, 1], in0=flat, scalar=0.5, in1=flat, op0=ALU.is_gt, op1=ALU.subtract
        )
        nc.vector.tensor_scalar(out=qflat, in0=flat, scalar1=0.25, scalar2=None, op0=ALU.add)
        nc.vector.scalar_tensor_tensor(
            out=arg[:, 0, :, 0], in0=qflat, scalar=0.5, in1=qflat, op0=ALU.is_gt, op1=ALU.subtract
        )
        nc.gpsimd.tensor_scalar(
            out=arg[:, 1, :, 0], in0=arg[:, 0, :, 1], scalar1=-1.0, scalar2=0.0, op0=ALU.mult, op1=ALU.add
        )
        nc.gpsimd.tensor_scalar(
            out=arg[:, 1, :, 1], in0=arg[:, 0, :, 0], scalar1=1.0, scalar2=0.0, op0=ALU.mult, op1=ALU.add
        )

        def make_table():
            nc.scalar.activation(
                out=table[:].rearrange("p a j c -> p (a j c)"),
                in_=arg[:].rearrange("p a n e -> p (a n e)"),
                func=ACTF.Sin, scale=-2.0 * PI,
            )

        results = []
        for b in range(BATCH):
            ob = opool.tile([P, SLOTS, FEATS], F32, name="ob%d" % b)
            results.append(ob)

        units = []
        for b in range(BATCH):
            for j0 in range(0, SLOTS, ROUND):
                units.append((b, j0, ROUND))
        units = units[:-1] + [(BATCH - 1, 12, 2), (BATCH - 1, 14, 2)]
        stores = {}
        for b in range(BATCH - 1):
            stores[(b, 12)] = (0, SLOTS)
        stores[(BATCH - 1, 4)] = (0, 8)
        stores[(BATCH - 1, 8)] = (8, 4)
        stores[(BATCH - 1, 12)] = (12, 2)
        stores[(BATCH - 1, 14)] = (14, 2)

        grouped = {}
        quantised = {}

        reordered = {}

        def reorder(u):
            b, j0, n = units[u]
            m = REORDERED
            xs, jj = where[(b, j0 + n - m)]
            xp = ppool.tile([P, m * WORDS], F32, name="xp", tag="xp", align_bytes=64)
            nc.vector.tensor_copy(
                out=xp[:].rearrange("p (g u c) -> p g u c", u=2, c=P),
                in_=xs[:].bitcast(F32)[:, jj * WORDS : (jj + m) * WORDS].rearrange("p (g c u) -> p g u c", u=2, c=P),
            )
            for t in range(m):
                reordered[(u, n - m + t)] = (xp, t)

        def transpose_and_copy(u):
            b, j0, n = units[u]
            grp = gpool.tile([P, n * WORDS], F32, name="grp", tag="grp", align_bytes=64)
            grouped[u] = grp
            for t in range(n):
                xs, jj = where[(b, j0 + t)]
                xw = xs[:].bitcast(F32)
                xt = psx.tile([P, WORDS], F32, name="xt", tag="xt")
                for a in range(4):
                    if (u, t) in reordered:
                        xp, tp = reordered[(u, t)]
                        words = xp[:, tp * WORDS + a * P : tp * WORDS + (a + 1) * P]
                    else:
                        first = jj * WORDS + (a // 2) * 2 * P + a % 2
                        words = xw[:, first : (jj * WORDS + (a // 2 + 1) * 2 * P) : 2]
                    nc.tensor.transpose(xt[:, a * P : (a + 1) * P], words, ident[:])
                nc.scalar.copy(
                    out=grp[:, t * WORDS : (t + 1) * WORDS].rearrange("p (g r u) -> p g r u", g=2, u=2),
                    in_=xt[:].rearrange("p (g u r) -> p g r u", g=2, u=2),
                )
                if t == 1 and u - 3 >= 0:
                    pass_through(u - 3)
                if u == 0 and t == 1:
                    regroup_w()
                if u == 2 and t == 1:
                    make_table()

        def quantise(u):
            n = units[u][2]
            codes = qpool.tile([P, n * 2 * P], U32, name="codes", tag="codes", align_bytes=64)
            scales = qpool.tile([P, n * 2 * P], U8, name="scales", tag="scales", align_bytes=64)
            nc.vector.quantize_mx(
                out=codes[:].bitcast(FP8X4), scales=scales[:], in_=grouped[u][:].bitcast(BF16)
            )
            quantised[u] = (codes, scales)

        rotating = {}

        def multiply_and_rotate(u):
            b, j0, n = units[u]
            codes, scales = quantised[u]
            acc = psa.tile([P, n * FEATS], F32, name="acc", tag="acc")
            for t in range(n):
                for g in range(2):
                    cols = slice((2 * t + g) * P, (2 * t + g + 1) * P)
                    nc.tensor.matmul_mx(
                        out=acc[:, t * FEATS : (t + 1) * FEATS],
                        lhsT=codes[:, cols].bitcast(FP8X4),
                        lhsT_scale=scales[:, cols],
                        rhs=w_codes[:, g * FEATS : (g + 1) * FEATS].bitcast(FP8X4),
                        rhs_scale=w_scales[:, g * FEATS : (g + 1) * FEATS],
                        start=(g == 0),
                        stop=(g == 1),
                    )
            q = acc[:].rearrange("p (t h d) -> p t h d", t=n, h=HEADS)
            o = results[b][:, j0 : j0 + n, :].rearrange("p t (h d) -> p t h d", h=HEADS)
            shape = [P, n, HEADS, PAIRS, 2]
            pairs = q[:, :, :, NOPE:HEAD_DIM].rearrange("p t h (i e) -> p t h i e", e=2)
            o_rope = o[:, :, :, NOPE:HEAD_DIM].rearrange("p t h (i e) -> p t h i e", e=2)
            v = vpool.tile(shape, F32, name="v", tag="v")
            nc.vector.tensor_tensor(
                out=o_rope,
                in0=pairs[:, :, :, :, 0:1].to_broadcast(shape),
                in1=table[:, 0, j0 : j0 + n, :].rearrange("p t (i e) -> p t i e", e=2)
                .unsqueeze(2).to_broadcast(shape),
                op=ALU.mult,
            )
            nc.vector.tensor_tensor(
                out=v[:],
                in0=pairs[:, :, :, :, 1:2].to_broadcast(shape),
                in1=table[:, 1, j0 : j0 + n, :].rearrange("p t (i e) -> p t i e", e=2)
                .unsqueeze(2).to_broadcast(shape),
                op=ALU.mult,
            )
            rotating[u] = (q, o, o_rope, v)

        def pass_through(u):
            q, o, o_rope, v = rotating[u]
            nc.scalar.copy(out=o[:, :, :, 0:NOPE], in_=q[:, :, :, 0:NOPE])

        def add_and_store(u):
            b, j0, n = units[u]
            q, o, o_rope, v = rotating[u]
            nc.vector.tensor_tensor(out=o_rope, in0=o_rope, in1=v[:], op=ALU.add)
            if (b, j0) in stores:
                s0, sn = stores[(b, j0)]
                nc.sync.dma_start(
                    out=out[b].rearrange("(p j) h d -> p j (h d)", j=SLOTS)[:, s0 : s0 + sn, :],
                    in_=results[b][:, s0 : s0 + sn, :],
                )

        for u in range(-2, len(units)):
            if u + 2 < len(units):
                transpose_and_copy(u + 2)
            elif u >= 1:
                pass_through(u - 1)
            if u == -2:
                quantise_w()
            if 0 <= u + 1 < len(units):
                quantise(u + 1)
            if u >= 1:
                add_and_store(u - 1)
            if 3 <= u + 3 < len(units) - 2:
                reorder(u + 3)
            if u >= 0:
                multiply_and_rotate(u)
        pass_through(len(units) - 1)
        add_and_store(len(units) - 1)
